import numpy as np
import ml_dtypes


def mxq(x, axis, fmt="e4m3"):
    dtype, down = {"e4m3": (ml_dtypes.float8_e4m3fn, 7), "e5m2": (ml_dtypes.float8_e5m2, 14)}[fmt]
    v = np.moveaxis(np.asarray(x, np.float32).astype(ml_dtypes.bfloat16).astype(np.float64), axis, -1)
    blocks = v.reshape(v.shape[:-1] + (-1, 32))
    amax = np.abs(blocks).max(-1, keepdims=True)
    byte = np.maximum(np.where(amax > 0, np.frexp(amax)[1] - 1 + 127, 0) - down, 1)
    scale = np.exp2(byte - 127.0)
    codes = (blocks / scale).astype(np.float32).astype(dtype).astype(np.float64)
    return np.moveaxis((codes * scale).reshape(v.shape), -1, axis)


WIDE = False


def mx_kscale(k):
    if not WIDE:
        return np.ones(k)
    levels = np.array([10, -10, 5, -5, 0])
    if k % 512:
        return np.exp2(np.random.permutation(np.resize(levels, k // 32))).repeat(32)
    a = np.empty((k // 512, 16))
    for p in range(k // 512):
        a[p, :8] = np.random.permutation(np.resize(levels, 8))
        for g in range(8):
            far = levels[np.abs(levels - a[p, g]) >= 10]
            a[p, g + 8] = far[np.random.randint(len(far))]
    return np.exp2(a.ravel()).repeat(32)


BF16 = ml_dtypes.bfloat16


def bf(x):
    return np.asarray(x, np.float32).astype(BF16)


def f64(x):
    return np.asarray(x).astype(np.float64)


S, E = 1536, 1024


def setup_inputs():
    s, t = mx_kscale(E), mx_kscale(S)
    return {"qm": bf(np.random.standard_normal((S, E)) * 0.4 * s),
            "km": bf(np.random.standard_normal((S, E)) * 0.4 / s * t[:, None]),
            "vm": bf(np.random.standard_normal((S, E)) * 0.4 / t[:, None])}


def reference(qm, km, vm):
    qkm = (mxq(f64(qm), 1, "e4m3") @ mxq(f64(km), 1, "e4m3").T) / np.sqrt(S)
    z = mxq(qkm, 1, "e4m3") @ mxq(f64(vm), 0, "e4m3")
    e = np.exp(z - z.max(-1, keepdims=True))
    return e / e.sum(-1, keepdims=True)

@@ -1,0 +1,277 @@
+import math
+from contextlib import ExitStack
+
+import concourse.mybir as mybir
+from concourse.masks import make_identity
+
+F32 = mybir.dt.float32
+BF16 = mybir.dt.bfloat16
+U32 = mybir.dt.uint32
+U8 = mybir.dt.uint8
+FP8X4 = mybir.dt.float8_e4m3fn_x4
+ACT = mybir.ActivationFunctionType
+ALU = mybir.AluOpType
+AXIS = mybir.AxisListType
+
+S = 1536
+E = 1024
+P = 128
+PACK = 4
+K_PASS = P * PACK
+BANK = 512
+
+GROUPS = S // K_PASS
+TILES = K_PASS // P
+E_PASSES = E // K_PASS
+HALVES = E // BANK
+TILE_WORDS = E // PACK
+LAG = 2
+
+FLOPS = 2 * S * S * E + 2 * S * S * E
+
+
+def tile_headattetion_pa_kernel(tc, qm, km, vm, out):
+    nc = tc.nc
+    inv_sqrt_s = 1.0 / math.sqrt(S)
+
+    with ExitStack() as ctx:
+        const = ctx.enter_context(tc.tile_pool(name="const", bufs=1))
+        keep = ctx.enter_context(tc.tile_pool(name="keep", bufs=1))
+        raw_pool = ctx.enter_context(tc.tile_pool(name="raw", bufs=3 * GROUPS))
+        stage = ctx.enter_context(tc.tile_pool(name="stage", bufs=3))
+        rows = ctx.enter_context(tc.tile_pool(name="rows", bufs=6))
+        small = ctx.enter_context(tc.tile_pool(name="small", bufs=6))
+        psum = ctx.enter_context(tc.psum_pool(name="psum", bufs=8))
+        ctx.enter_context(tc.manual_schedule())
+
+        k_codes = keep.tile([P, GROUPS * TILES * TILE_WORDS], U32, align_bytes=64)
+        k_scales = keep.tile([P, GROUPS * TILES * TILE_WORDS], U8, align_bytes=64)
+        q_codes = keep.tile([P, GROUPS * TILES * TILE_WORDS], U32, align_bytes=64)
+        q_scales = keep.tile([P, GROUPS * TILES * TILE_WORDS], U8, align_bytes=64)
+        v_codes = keep.tile([P, GROUPS * E], U32, align_bytes=64)
+        v_scales = keep.tile([P, GROUPS * E], U8, align_bytes=64)
+        s_codes = keep.tile([P, GROUPS * S], U32, align_bytes=64)
+        s_scales = keep.tile([P, GROUPS * S], U8, align_bytes=64)
+
+        blocks = [(c, g) for g in range(GROUPS) for c in range(GROUPS)]
+        needs = []
+        for c, g in blocks:
+            for operand in (("k", c), ("q", g)):
+                if operand not in needs:
+                    needs.append(operand)
+
+        raw_tiles = {}
+        for kind, group in needs:
+            src = km if kind == "k" else qm
+            raw = raw_pool.tile([P, TILES * E], BF16, name="raw_%s%d" % (kind, group), tag="raw")
+            tiles = src[group * K_PASS : (group + 1) * K_PASS, :].rearrange(
+                "(p t) e -> t p e", t=TILES
+            )
+            for t in range(TILES):
+                nc.sync.dma_start(out=raw[:, t * E : (t + 1) * E], in_=tiles[t])
+            raw_tiles[(kind, group)] = raw
+        for group in range(GROUPS):
+            raw = raw_pool.tile([P, TILES * E], BF16, name="raw_v%d" % group, tag="raw")
+            nc.sync.dma_start(
+                out=raw[:],
+                in_=vm[group * K_PASS : (group + 1) * K_PASS, :].rearrange(
+                    "(p t) e -> p (t e)", t=TILES
+                ),
+            )
+            raw_tiles[("v", group)] = raw
+
+        ident = const.tile([P, P], F32)
+        make_identity(nc, ident[:])
+
+        warm = const.tile([P, 1], F32)
+        nc.vector.memset(warm[:], 0.0)
+        nc.scalar.activation(out=warm[:], in_=warm[:], func=ACT.Exp)
+
+        def prepare(kind, group):
+            raw_words = raw_tiles[(kind, group)][:].bitcast(F32)
+            codes, scales = (k_codes, k_scales) if kind == "k" else (q_codes, q_scales)
+            grouped = stage.tile([P, TILES * E], BF16, tag="grouped", align_bytes=64)
+            grouped_words = grouped[:].bitcast(F32)
+            words = E // 2
+            for t in range(TILES):
+                bank = psum.tile([P, BANK], F32, name="bank_t", tag="bank")
+                for j in range(words // P):
+                    first_word = t * words + 2 * P * (j // 2) + j % 2
+                    nc.tensor.transpose(
+                        bank[:, j * P : (j + 1) * P],
+                        raw_words[:, first_word : first_word + 2 * P - 1 : 2],
+                        ident[:],
+                    )
+                dst = grouped_words[:, t * words : (t + 1) * words].rearrange(
+                    "p (a r u) -> p a r u", a=E_PASSES, u=2
+                )
+                src = bank[:].rearrange("p (a u r) -> p a r u", a=E_PASSES, u=2)
+                if t % 2 == 0:
+                    nc.scalar.copy(out=dst, in_=src)
+                else:
+                    nc.vector.tensor_copy(out=dst, in_=src)
+            for t in range(TILES):
+                first = (group * TILES + t) * TILE_WORDS
+                nc.vector.quantize_mx(
+                    out=codes[:, first : first + TILE_WORDS].bitcast(FP8X4),
+                    scales=scales[:, first : first + TILE_WORDS],
+                    in_=grouped[:, t * E : (t + 1) * E],
+                )
+
+        def score_block(c, g):
+            s_grouped = stage.tile([P, TILES * P * PACK], BF16, tag="s_grouped", align_bytes=64)
+            for i in range(TILES):
+                bank = psum.tile([P, BANK], F32, name="bank_s", tag="bank")
+                for t in range(TILES):
+                    for a in range(E_PASSES):
+                        k_first = (c * TILES + t) * TILE_WORDS + a * P
+                        q_first = (g * TILES + i) * TILE_WORDS + a * P
+                        nc.tensor.matmul_mx(
+                            out=bank[:, t * P : (t + 1) * P],
+                            lhsT=k_codes[:, k_first : k_first + P].bitcast(FP8X4),
+                            lhsT_scale=k_scales[:, k_first : k_first + P],
+                            rhs=q_codes[:, q_first : q_first + P].bitcast(FP8X4),
+                            rhs_scale=q_scales[:, q_first : q_first + P],
+                            start=(a == 0),
+                            stop=(a == E_PASSES - 1),
+                        )
+                nc.scalar.activation(
+                    out=s_grouped[:, i * BANK : (i + 1) * BANK].rearrange(
+                        "p (n t) -> p n t", t=TILES
+                    ),
+                    in_=bank[:].rearrange("p (t n) -> p n t", t=TILES),
+                    func=ACT.Copy,
+                    scale=inv_sqrt_s,
+                )
+            return s_grouped
+
+        def quantise_block(c, g, s_grouped):
+            first = (c * GROUPS + g) * K_PASS
+            nc.vector.quantize_mx(
+                out=s_codes[:, first : first + K_PASS].bitcast(FP8X4),
+                scales=s_scales[:, first : first + K_PASS],
+                in_=s_grouped[:],
+            )
+
+        def regroup_v(c, h):
+            v_grouped = stage.tile([P, BANK * PACK], BF16, tag="v_grouped", align_bytes=64)
+            src = raw_tiles[("v", c)][:].rearrange("p (t f) -> p t f", t=TILES)
+            nc.vector.tensor_copy(
+                out=v_grouped[:].rearrange("p (b i t) -> p b t i", i=4, t=TILES),
+                in_=src[:, :, h * BANK : (h + 1) * BANK].rearrange("p t (b i) -> p b t i", i=4),
+            )
+            return v_grouped
+
+        def quantise_v(c, h, v_grouped):
+            first = c * E + h * BANK
+            nc.vector.quantize_mx(
+                out=v_codes[:, first : first + BANK].bitcast(FP8X4),
+                scales=v_scales[:, first : first + BANK],
+                in_=v_grouped[:],
+            )
+
+        v_pieces = [(c, h) for c in range(GROUPS) for h in range(HALVES)]
+        first_v_block = len(blocks) - len(v_pieces) - 1
+        prepare(*needs[0])
+        prepare(*needs[1])
+        waiting = None
+        for b, (c, g) in enumerate(blocks):
+            if b + 2 < len(needs):
+                prepare(*needs[b + 2])
+            s_grouped = score_block(c, g)
+            piece = b - first_v_block
+            if 0 <= piece < len(v_pieces):
+                v_grouped = regroup_v(*v_pieces[piece])
+            if waiting is not None:
+                quantise_block(*waiting)
+            if 0 <= piece < len(v_pieces):
+                quantise_v(*v_pieces[piece], v_grouped)
+            waiting = (c, g, s_grouped)
+        quantise_block(*waiting)
+
+        out_tiles = out.rearrange("(g p t) f -> g t p f", p=P, t=TILES)
+
+        def z_passes(g, i):
+            z = [psum.tile([P, BANK], F32, name="bank_z%d" % h, tag="bank") for h in range(HALVES)]
+            for h in range(HALVES):
+                for c in range(GROUPS):
+                    s_first = (c * GROUPS + g) * K_PASS + i * P
+                    v_first = c * E + h * BANK
+                    nc.tensor.matmul_mx(
+                        out=z[h][:],
+                        lhsT=s_codes[:, s_first : s_first + P].bitcast(FP8X4),
+                        lhsT_scale=s_scales[:, s_first : s_first + P],
+                        rhs=v_codes[:, v_first : v_first + BANK].bitcast(FP8X4),
+                        rhs_scale=v_scales[:, v_first : v_first + BANK],
+                        start=(c == 0),
+                        stop=(c == GROUPS - 1),
+                    )
+            return z
+
+        def maxima_of_halves(z):
+            half_max = small.tile([P, HALVES], F32, tag="half_max")
+            for h in range(HALVES):
+                nc.vector.tensor_reduce(
+                    out=half_max[:, h : h + 1], in_=z[h][:], axis=AXIS.X, op=ALU.max
+                )
+            return half_max
+
+        def exponentials(z, half_max):
+            neg_max = small.tile([P, 1], F32, tag="neg_max")
+            nc.vector.tensor_reduce(
+                out=neg_max[:], in_=half_max[:], axis=AXIS.X, op=ALU.max, negate=True
+            )
+            e_row = rows.tile([P, E], F32, tag="e_row")
+            half_sum = small.tile([P, HALVES], F32, tag="half_sum")
+            for h in range(HALVES):
+                nc.scalar.activation(
+                    out=e_row[:, h * BANK : (h + 1) * BANK],
+                    in_=z[h][:],
+                    func=ACT.Exp,
+                    bias=neg_max[:, 0:1],
+                    scale=1.0,
+                    accum_out=half_sum[:, h : h + 1],
+                )
+            return e_row, half_sum
+
+        def sum_of_halves(half_sum):
+            total = small.tile([P, 1], F32, tag="total")
+            nc.vector.tensor_reduce(out=total[:], in_=half_sum[:], axis=AXIS.X, op=ALU.add)
+            return total
+
+        def normalise_and_store(g, i, e_row, total, vector_is_free):
+            inverse = small.tile([P, 1], F32, tag="inverse")
+            nc.vector.reciprocal(out=inverse[:], in_=total[:])
+            if not vector_is_free:
+                nc.gpsimd.tensor_scalar(
+                    out=e_row[:],
+                    in0=e_row[:],
+                    scalar1=inverse[:, 0:1],
+                    scalar2=0.0,
+                    op0=ALU.mult,
+                    op1=ALU.add,
+                )
+                nc.sync.dma_start(out=out_tiles[g, i], in_=e_row[:])
+            else:
+                for h in range(HALVES):
+                    cols = slice(h * BANK, (h + 1) * BANK)
+                    nc.vector.tensor_scalar_mul(
+                        out=e_row[:, cols], in0=e_row[:, cols], scalar1=inverse[:, 0:1]
+                    )
+                    nc.sync.dma_start(out=out_tiles[g, i][:, cols], in_=e_row[:, cols])
+
+        query_tiles = [(g, i) for g in range(GROUPS) for i in range(TILES)]
+        issued = []
+        for n in range(len(query_tiles) + LAG):
+            old = issued[n - LAG] if n >= LAG else None
+            if n < len(query_tiles):
+                g, i = query_tiles[n]
+                z = z_passes(g, i)
+                half_max = maxima_of_halves(z)
+            if old is not None:
+                total = sum_of_halves(old[3])
+            if n < len(query_tiles):
+                e_row, half_sum = exponentials(z, half_max)
+                issued.append((g, i, e_row, half_sum))
+            if old is not None:
+                normalise_and_store(old[0], old[1], old[2], total, n >= len(query_tiles))

@@ -25,7 +25,6 @@ TILES = K_PASS // P
 E_PASSES = E // K_PASS
 HALVES = E // BANK
 TILE_WORDS = E // PACK
-LAG = 2
 
 FLOPS = 2 * S * S * E + 2 * S * S * E
 
@@ -261,17 +260,13 @@ def tile_headattetion_pa_kernel(tc, qm, km, vm, out):
                     nc.sync.dma_start(out=out_tiles[g, i][:, cols], in_=e_row[:, cols])
 
         query_tiles = [(g, i) for g in range(GROUPS) for i in range(TILES)]
-        issued = []
-        for n in range(len(query_tiles) + LAG):
-            old = issued[n - LAG] if n >= LAG else None
-            if n < len(query_tiles):
-                g, i = query_tiles[n]
-                z = z_passes(g, i)
-                half_max = maxima_of_halves(z)
+        old = None
+        for n, (g, i) in enumerate(query_tiles):
+            z = z_passes(g, i)
+            half_max = maxima_of_halves(z)
+            e_row, half_sum = exponentials(z, half_max)
             if old is not None:
-                total = sum_of_halves(old[3])
-            if n < len(query_tiles):
-                e_row, half_sum = exponentials(z, half_max)
-                issued.append((g, i, e_row, half_sum))
-            if old is not None:
-                normalise_and_store(old[0], old[1], old[2], total, n >= len(query_tiles))
+                last = n == len(query_tiles) - 1
+                normalise_and_store(old[0], old[1], old[2], sum_of_halves(old[3]), last)
+            old = (g, i, e_row, half_sum)
+        normalise_and_store(old[0], old[1], old[2], sum_of_halves(old[3]), True)

@@ -24,6 +24,7 @@ GROUPS = S // K_PASS
 TILES = K_PASS // P
 E_PASSES = E // K_PASS
 HALVES = E // BANK
+FIRST_V_BLOCK = 3
 TILE_WORDS = E // PACK
 
 FLOPS = 2 * S * S * E + 2 * S * S * E
@@ -40,6 +41,7 @@ def tile_headattetion_pa_kernel(tc, qm, km, vm, out):
         stage = ctx.enter_context(tc.tile_pool(name="stage", bufs=3))
         rows = ctx.enter_context(tc.tile_pool(name="rows", bufs=6))
         small = ctx.enter_context(tc.tile_pool(name="small", bufs=6))
+        straight = ctx.enter_context(tc.tile_pool(name="straight", bufs=8))
         psum = ctx.enter_context(tc.psum_pool(name="psum", bufs=8))
         ctx.enter_context(tc.manual_schedule())
 
@@ -86,29 +88,47 @@ def tile_headattetion_pa_kernel(tc, qm, km, vm, out):
         nc.vector.memset(warm[:], 0.0)
         nc.scalar.activation(out=warm[:], in_=warm[:], func=ACT.Exp)
 
-        def prepare(kind, group):
+        words = E // 2
+        straightened = {}
+        grouped_tiles = {}
+
+        def straighten(kind, group):
             raw_words = raw_tiles[(kind, group)][:].bitcast(F32)
-            codes, scales = (k_codes, k_scales) if kind == "k" else (q_codes, q_scales)
+            straightened[(kind, group)] = []
+            for t in range(TILES):
+                tile = straight.tile([P, words], F32, name="straight_t", tag="straight", align_bytes=64)
+                nc.vector.tensor_copy(
+                    out=tile[:].rearrange("p (u w) -> p u w", u=2),
+                    in_=raw_words[:, t * words : (t + 1) * words].rearrange("p (w u) -> p u w", u=2),
+                )
+                straightened[(kind, group)].append(tile)
+
+        def transpose_group(kind, group):
+            raw_words = raw_tiles[(kind, group)][:].bitcast(F32)
             grouped = stage.tile([P, TILES * E], BF16, tag="grouped", align_bytes=64)
             grouped_words = grouped[:].bitcast(F32)
-            words = E // 2
             for t in range(TILES):
                 bank = psum.tile([P, BANK], F32, name="bank_t", tag="bank")
                 for j in range(words // P):
-                    first_word = t * words + 2 * P * (j // 2) + j % 2
-                    nc.tensor.transpose(
-                        bank[:, j * P : (j + 1) * P],
-                        raw_words[:, first_word : first_word + 2 * P - 1 : 2],
-                        ident[:],
-                    )
-                dst = grouped_words[:, t * words : (t + 1) * words].rearrange(
-                    "p (a r u) -> p a r u", a=E_PASSES, u=2
+                    a, u = j // 2, j % 2
+                    if (kind, group) in straightened:
+                        first = u * (words // 2) + a * P
+                        in_ = straightened[(kind, group)][t][:, first : first + P]
+                    else:
+                        first = t * words + 2 * P * a + u
+                        in_ = raw_words[:, first : first + 2 * P - 1 : 2]
+                    nc.tensor.transpose(bank[:, j * P : (j + 1) * P], in_, ident[:])
+                nc.scalar.copy(
+                    out=grouped_words[:, t * words : (t + 1) * words].rearrange(
+                        "p (a r u) -> p a r u", a=E_PASSES, u=2
+                    ),
+                    in_=bank[:].rearrange("p (a u r) -> p a r u", a=E_PASSES, u=2),
                 )
-                src = bank[:].rearrange("p (a u r) -> p a r u", a=E_PASSES, u=2)
-                if t % 2 == 0:
-                    nc.scalar.copy(out=dst, in_=src)
-                else:
-                    nc.vector.tensor_copy(out=dst, in_=src)
+            grouped_tiles[(kind, group)] = grouped
+
+        def quantise_group(kind, group):
+            codes, scales = (k_codes, k_scales) if kind == "k" else (q_codes, q_scales)
+            grouped = grouped_tiles[(kind, group)]
             for t in range(TILES):
                 first = (group * TILES + t) * TILE_WORDS
                 nc.vector.quantize_mx(
@@ -170,21 +190,24 @@ def tile_headattetion_pa_kernel(tc, qm, km, vm, out):
             )
 
         v_pieces = [(c, h) for c in range(GROUPS) for h in range(HALVES)]
-        first_v_block = len(blocks) - len(v_pieces) - 1
-        prepare(*needs[0])
-        prepare(*needs[1])
+        for n in range(2):
+            transpose_group(*needs[n])
+            quantise_group(*needs[n])
         waiting = None
         for b, (c, g) in enumerate(blocks):
             if b + 2 < len(needs):
-                prepare(*needs[b + 2])
+                transpose_group(*needs[b + 2])
             s_grouped = score_block(c, g)
-            piece = b - first_v_block
-            if 0 <= piece < len(v_pieces):
-                v_grouped = regroup_v(*v_pieces[piece])
+            pieces = v_pieces[b - FIRST_V_BLOCK : b - FIRST_V_BLOCK + 1] if b >= FIRST_V_BLOCK else []
+            v_grouped = [regroup_v(*piece) for piece in pieces]
             if waiting is not None:
                 quantise_block(*waiting)
-            if 0 <= piece < len(v_pieces):
-                quantise_v(*v_pieces[piece], v_grouped)
+            if b + 2 < len(needs):
+                quantise_group(*needs[b + 2])
+            for piece, tile in zip(pieces, v_grouped):
+                quantise_v(*piece, tile)
+            if b + 3 < len(needs):
+                straighten(*needs[b + 3])
             waiting = (c, g, s_grouped)
         quantise_block(*waiting)
 
@@ -259,14 +282,82 @@ def tile_headattetion_pa_kernel(tc, qm, km, vm, out):
                     )
                     nc.sync.dma_start(out=out_tiles[g, i][:, cols], in_=e_row[:, cols])
 
+        def last_tile(g, i, old):
+            edges = [0, BANK, BANK + BANK // 2, E]
+            z = []
+            for h in range(3):
+                width = edges[h + 1] - edges[h]
+                bank = psum.tile([P, BANK], F32, name="bank_l%d" % h, tag="bank")
+                for c in range(GROUPS):
+                    s_first = (c * GROUPS + g) * K_PASS + i * P
+                    v_first = c * E + edges[h]
+                    nc.tensor.matmul_mx(
+                        out=bank[:, 0:width],
+                        lhsT=s_codes[:, s_first : s_first + P].bitcast(FP8X4),
+                        lhsT_scale=s_scales[:, s_first : s_first + P],
+                        rhs=v_codes[:, v_first : v_first + width].bitcast(FP8X4),
+                        rhs_scale=v_scales[:, v_first : v_first + width],
+                        start=(c == 0),
+                        stop=(c == GROUPS - 1),
+                    )
+                z.append(bank[:, 0:width])
+            neg_maxima = small.tile([P, 3], F32, tag="neg_maxima")
+            neg_max = small.tile([P, 1], F32, tag="neg_max")
+            e_row = rows.tile([P, E], F32, tag="e_row")
+            sums = small.tile([P, 4], F32, tag="sums")
+
+            def exponentials_of(h, bias):
+                nc.scalar.activation(
+                    out=e_row[:, edges[h] : edges[h + 1]],
+                    in_=z[h],
+                    func=ACT.Exp,
+                    bias=bias,
+                    scale=1.0,
+                    accum_out=sums[:, h : h + 1],
+                )
+
+            for h in range(3):
+                nc.vector.tensor_reduce(
+                    out=neg_maxima[:, h : h + 1], in_=z[h], axis=AXIS.X, op=ALU.max, negate=True
+                )
+                if h == 0:
+                    exponentials_of(0, neg_maxima[:, 0:1])
+            nc.vector.tensor_reduce(out=neg_max[:], in_=neg_maxima[:], axis=AXIS.X, op=ALU.min)
+            correction = small.tile([P, 1], F32, tag="correction")
+            nc.scalar.activation(
+                out=correction[:], in_=neg_maxima[:, 0:1], func=ACT.Exp, bias=neg_max[:, 0:1], scale=-1.0
+            )
+            normalise_and_store(old[0], old[1], old[2], sum_of_halves(old[3]), True)
+            exponentials_of(1, neg_max[:, 0:1])
+            exponentials_of(2, neg_max[:, 0:1])
+            total = small.tile([P, 1], F32, tag="total")
+            nc.vector.scalar_tensor_tensor(
+                out=sums[:, 3:4], in0=sums[:, 0:1], scalar=correction[:, 0:1], in1=sums[:, 1:2], op0=ALU.mult, op1=ALU.add
+            )
+            nc.vector.tensor_tensor(out=total[:], in0=sums[:, 2:3], in1=sums[:, 3:4], op=ALU.add)
+            inverse = small.tile([P, 1], F32, tag="inverse")
+            nc.vector.reciprocal(out=inverse[:], in_=total[:])
+            cut = BANK + BANK // 4
+            nc.scalar.activation(out=e_row[:, cut:E], in_=e_row[:, cut:E], func=ACT.Copy, scale=inverse[:, 0:1])
+            nc.vector.tensor_scalar(
+                out=e_row[:, 0:BANK],
+                in0=e_row[:, 0:BANK],
+                scalar1=correction[:, 0:1],
+                scalar2=inverse[:, 0:1],
+                op0=ALU.mult,
+                op1=ALU.mult,
+            )
+            nc.sync.dma_start(out=out_tiles[g, i][:, 0:BANK], in_=e_row[:, 0:BANK])
+            nc.vector.tensor_scalar_mul(out=e_row[:, BANK:cut], in0=e_row[:, BANK:cut], scalar1=inverse[:, 0:1])
+            nc.sync.dma_start(out=out_tiles[g, i][:, BANK:E], in_=e_row[:, BANK:E])
+
         query_tiles = [(g, i) for g in range(GROUPS) for i in range(TILES)]
         old = None
-        for n, (g, i) in enumerate(query_tiles):
+        for g, i in query_tiles[:-1]:
             z = z_passes(g, i)
             half_max = maxima_of_halves(z)
             e_row, half_sum = exponentials(z, half_max)
             if old is not None:
-                last = n == len(query_tiles) - 1
-                normalise_and_store(old[0], old[1], old[2], sum_of_halves(old[3]), last)
+                normalise_and_store(old[0], old[1], old[2], sum_of_halves(old[3]), False)
             old = (g, i, e_row, half_sum)
-        normalise_and_store(old[0], old[1], old[2], sum_of_halves(old[3]), True)
+        last_tile(*query_tiles[-1], old)

@@ -24,7 +24,7 @@ GROUPS = S // K_PASS
 TILES = K_PASS // P
 E_PASSES = E // K_PASS
 HALVES = E // BANK
-FIRST_V_BLOCK = 3
+HEAD = 3
 TILE_WORDS = E // PACK
 
 FLOPS = 2 * S * S * E + 2 * S * S * E
@@ -92,50 +92,48 @@ def tile_headattetion_pa_kernel(tc, qm, km, vm, out):
         straightened = {}
         grouped_tiles = {}
 
-        def straighten(kind, group):
+        def straighten(kind, group, t):
             raw_words = raw_tiles[(kind, group)][:].bitcast(F32)
-            straightened[(kind, group)] = []
-            for t in range(TILES):
-                tile = straight.tile([P, words], F32, name="straight_t", tag="straight", align_bytes=64)
-                nc.vector.tensor_copy(
-                    out=tile[:].rearrange("p (u w) -> p u w", u=2),
-                    in_=raw_words[:, t * words : (t + 1) * words].rearrange("p (w u) -> p u w", u=2),
-                )
-                straightened[(kind, group)].append(tile)
+            tile = straight.tile([P, words], F32, name="straight_t", tag="straight", align_bytes=64)
+            nc.vector.tensor_copy(
+                out=tile[:].rearrange("p (u w) -> p u w", u=2),
+                in_=raw_words[:, t * words : (t + 1) * words].rearrange("p (w u) -> p u w", u=2),
+            )
+            straightened[(kind, group, t)] = tile
 
-        def transpose_group(kind, group):
+        def transpose_tile(kind, group, t):
             raw_words = raw_tiles[(kind, group)][:].bitcast(F32)
-            grouped = stage.tile([P, TILES * E], BF16, tag="grouped", align_bytes=64)
-            grouped_words = grouped[:].bitcast(F32)
-            for t in range(TILES):
-                bank = psum.tile([P, BANK], F32, name="bank_t", tag="bank")
-                for j in range(words // P):
-                    a, u = j // 2, j % 2
-                    if (kind, group) in straightened:
-                        first = u * (words // 2) + a * P
-                        in_ = straightened[(kind, group)][t][:, first : first + P]
-                    else:
-                        first = t * words + 2 * P * a + u
-                        in_ = raw_words[:, first : first + 2 * P - 1 : 2]
-                    nc.tensor.transpose(bank[:, j * P : (j + 1) * P], in_, ident[:])
-                nc.scalar.copy(
-                    out=grouped_words[:, t * words : (t + 1) * words].rearrange(
-                        "p (a r u) -> p a r u", a=E_PASSES, u=2
-                    ),
-                    in_=bank[:].rearrange("p (a u r) -> p a r u", a=E_PASSES, u=2),
+            if t == 0:
+                grouped_tiles[(kind, group)] = stage.tile(
+                    [P, TILES * E], BF16, name="grouped", tag="grouped", align_bytes=64
                 )
-            grouped_tiles[(kind, group)] = grouped
+            grouped_words = grouped_tiles[(kind, group)][:].bitcast(F32)
+            bank = psum.tile([P, BANK], F32, name="bank_t", tag="bank")
+            for j in range(words // P):
+                a, u = j // 2, j % 2
+                if (kind, group, t) in straightened:
+                    first = u * (words // 2) + a * P
+                    in_ = straightened[(kind, group, t)][:, first : first + P]
+                else:
+                    first = t * words + 2 * P * a + u
+                    in_ = raw_words[:, first : first + 2 * P - 1 : 2]
+                nc.tensor.transpose(bank[:, j * P : (j + 1) * P], in_, ident[:])
+            copy = nc.scalar.copy if ("V" if t == 0 and (kind, group) not in needs[: HEAD - 1] else "S") == "S" else nc.vector.tensor_copy
+            copy(
+                out=grouped_words[:, t * words : (t + 1) * words].rearrange(
+                    "p (a r u) -> p a r u", a=E_PASSES, u=2
+                ),
+                in_=bank[:].rearrange("p (a u r) -> p a r u", a=E_PASSES, u=2),
+            )
 
-        def quantise_group(kind, group):
+        def quantise_tile(kind, group, t):
             codes, scales = (k_codes, k_scales) if kind == "k" else (q_codes, q_scales)
-            grouped = grouped_tiles[(kind, group)]
-            for t in range(TILES):
-                first = (group * TILES + t) * TILE_WORDS
-                nc.vector.quantize_mx(
-                    out=codes[:, first : first + TILE_WORDS].bitcast(FP8X4),
-                    scales=scales[:, first : first + TILE_WORDS],
-                    in_=grouped[:, t * E : (t + 1) * E],
-                )
+            first = (group * TILES + t) * TILE_WORDS
+            nc.vector.quantize_mx(
+                out=codes[:, first : first + TILE_WORDS].bitcast(FP8X4),
+                scales=scales[:, first : first + TILE_WORDS],
+                in_=grouped_tiles[(kind, group)][:, t * E : (t + 1) * E],
+            )
 
         def score_block(c, g):
             s_grouped = stage.tile([P, TILES * P * PACK], BF16, tag="s_grouped", align_bytes=64)
@@ -190,174 +188,145 @@ def tile_headattetion_pa_kernel(tc, qm, km, vm, out):
             )
 
         v_pieces = [(c, h) for c in range(GROUPS) for h in range(HALVES)]
-        for n in range(2):
-            transpose_group(*needs[n])
-            quantise_group(*needs[n])
+        head_tiles = [need + (t,) for need in needs[:HEAD] for t in range(TILES)]
+        for m, tile in enumerate(head_tiles):
+            transpose_tile(*tile)
+            if m >= 2:
+                quantise_tile(*head_tiles[m - 2])
+        for tile in head_tiles[-2:]:
+            quantise_tile(*tile)
         waiting = None
         for b, (c, g) in enumerate(blocks):
-            if b + 2 < len(needs):
-                transpose_group(*needs[b + 2])
+            ahead = needs[b + 2] if HEAD <= b + 2 < len(needs) else None
+            if ahead:
+                for t in range(TILES):
+                    transpose_tile(*ahead, t)
             s_grouped = score_block(c, g)
-            pieces = v_pieces[b - FIRST_V_BLOCK : b - FIRST_V_BLOCK + 1] if b >= FIRST_V_BLOCK else []
-            v_grouped = [regroup_v(*piece) for piece in pieces]
+            piece = b - (len(blocks) - len(v_pieces))
+            if piece >= 0:
+                v_grouped = regroup_v(*v_pieces[piece])
             if waiting is not None:
                 quantise_block(*waiting)
-            if b + 2 < len(needs):
-                quantise_group(*needs[b + 2])
-            for piece, tile in zip(pieces, v_grouped):
-                quantise_v(*piece, tile)
-            if b + 3 < len(needs):
-                straighten(*needs[b + 3])
+            if ahead:
+                for t in range(TILES):
+                    quantise_tile(*ahead, t)
+            if piece >= 0:
+                quantise_v(*v_pieces[piece], v_grouped)
+            if HEAD <= b + 3 < len(needs):
+                for t in range(TILES):
+                    straighten(*needs[b + 3], t)
             waiting = (c, g, s_grouped)
         quantise_block(*waiting)
 
         out_tiles = out.rearrange("(g p t) f -> g t p f", p=P, t=TILES)
 
-        def z_passes(g, i):
-            z = [psum.tile([P, BANK], F32, name="bank_z%d" % h, tag="bank") for h in range(HALVES)]
-            for h in range(HALVES):
+        def z_passes(g, i, edges):
+            banks = []
+            for lo, hi in zip(edges, edges[1:]):
+                bank = psum.tile([P, BANK], F32, name="bank_z", tag="bank")
                 for c in range(GROUPS):
                     s_first = (c * GROUPS + g) * K_PASS + i * P
-                    v_first = c * E + h * BANK
                     nc.tensor.matmul_mx(
-                        out=z[h][:],
+                        out=bank[:, 0 : hi - lo],
                         lhsT=s_codes[:, s_first : s_first + P].bitcast(FP8X4),
                         lhsT_scale=s_scales[:, s_first : s_first + P],
-                        rhs=v_codes[:, v_first : v_first + BANK].bitcast(FP8X4),
-                        rhs_scale=v_scales[:, v_first : v_first + BANK],
+                        rhs=v_codes[:, c * E + lo : c * E + hi].bitcast(FP8X4),
+                        rhs_scale=v_scales[:, c * E + lo : c * E + hi],
                         start=(c == 0),
                         stop=(c == GROUPS - 1),
                     )
-            return z
+                banks.append(bank[:, 0 : hi - lo])
+            return banks
 
-        def maxima_of_halves(z):
-            half_max = small.tile([P, HALVES], F32, tag="half_max")
-            for h in range(HALVES):
-                nc.vector.tensor_reduce(
-                    out=half_max[:, h : h + 1], in_=z[h][:], axis=AXIS.X, op=ALU.max
-                )
-            return half_max
-
-        def exponentials(z, half_max):
+        def exponentials(banks, edges):
+            n = len(banks)
+            neg_maxima = small.tile([P, 4], F32, tag="neg_maxima")
             neg_max = small.tile([P, 1], F32, tag="neg_max")
-            nc.vector.tensor_reduce(
-                out=neg_max[:], in_=half_max[:], axis=AXIS.X, op=ALU.max, negate=True
-            )
-            e_row = rows.tile([P, E], F32, tag="e_row")
-            half_sum = small.tile([P, HALVES], F32, tag="half_sum")
-            for h in range(HALVES):
-                nc.scalar.activation(
-                    out=e_row[:, h * BANK : (h + 1) * BANK],
-                    in_=z[h][:],
-                    func=ACT.Exp,
-                    bias=neg_max[:, 0:1],
-                    scale=1.0,
-                    accum_out=half_sum[:, h : h + 1],
-                )
-            return e_row, half_sum
-
-        def sum_of_halves(half_sum):
-            total = small.tile([P, 1], F32, tag="total")
-            nc.vector.tensor_reduce(out=total[:], in_=half_sum[:], axis=AXIS.X, op=ALU.add)
-            return total
-
-        def normalise_and_store(g, i, e_row, total, vector_is_free):
-            inverse = small.tile([P, 1], F32, tag="inverse")
-            nc.vector.reciprocal(out=inverse[:], in_=total[:])
-            if not vector_is_free:
-                nc.gpsimd.tensor_scalar(
-                    out=e_row[:],
-                    in0=e_row[:],
-                    scalar1=inverse[:, 0:1],
-                    scalar2=0.0,
-                    op0=ALU.mult,
-                    op1=ALU.add,
-                )
-                nc.sync.dma_start(out=out_tiles[g, i], in_=e_row[:])
-            else:
-                for h in range(HALVES):
-                    cols = slice(h * BANK, (h + 1) * BANK)
-                    nc.vector.tensor_scalar_mul(
-                        out=e_row[:, cols], in0=e_row[:, cols], scalar1=inverse[:, 0:1]
-                    )
-                    nc.sync.dma_start(out=out_tiles[g, i][:, cols], in_=e_row[:, cols])
-
-        def last_tile(g, i, old):
-            edges = [0, BANK, BANK + BANK // 2, E]
-            z = []
-            for h in range(3):
-                width = edges[h + 1] - edges[h]
-                bank = psum.tile([P, BANK], F32, name="bank_l%d" % h, tag="bank")
-                for c in range(GROUPS):
-                    s_first = (c * GROUPS + g) * K_PASS + i * P
-                    v_first = c * E + edges[h]
-                    nc.tensor.matmul_mx(
-                        out=bank[:, 0:width],
-                        lhsT=s_codes[:, s_first : s_first + P].bitcast(FP8X4),
-                        lhsT_scale=s_scales[:, s_first : s_first + P],
-                        rhs=v_codes[:, v_first : v_first + width].bitcast(FP8X4),
-                        rhs_scale=v_scales[:, v_first : v_first + width],
-                        start=(c == 0),
-                        stop=(c == GROUPS - 1),
-                    )
-                z.append(bank[:, 0:width])
-            neg_maxima = small.tile([P, 3], F32, tag="neg_maxima")
-            neg_max = small.tile([P, 1], F32, tag="neg_max")
-            e_row = rows.tile([P, E], F32, tag="e_row")
+            correction = small.tile([P, 1], F32, tag="correction")
             sums = small.tile([P, 4], F32, tag="sums")
-
-            def exponentials_of(h, bias):
+            e_row = rows.tile([P, E], F32, tag="e_row")
+            for h in range(n):
+                nc.vector.tensor_reduce(
+                    out=neg_maxima[:, h : h + 1], in_=banks[h], axis=AXIS.X, op=ALU.max, negate=True
+                )
+            nc.vector.tensor_reduce(
+                out=neg_max[:], in_=neg_maxima[:, 0:n], axis=AXIS.X, op=ALU.min
+            )
+            for h in range(n):
+                if h == 1:
+                    nc.scalar.activation(
+                        out=correction[:],
+                        in_=neg_maxima[:, 0:1],
+                        func=ACT.Exp,
+                        bias=neg_max[:, 0:1],
+                        scale=-1.0,
+                    )
                 nc.scalar.activation(
                     out=e_row[:, edges[h] : edges[h + 1]],
-                    in_=z[h],
+                    in_=banks[h],
                     func=ACT.Exp,
-                    bias=bias,
+                    bias=neg_maxima[:, 0:1] if h == 0 else neg_max[:, 0:1],
                     scale=1.0,
                     accum_out=sums[:, h : h + 1],
                 )
+            return e_row, correction, sums
 
-            for h in range(3):
-                nc.vector.tensor_reduce(
-                    out=neg_maxima[:, h : h + 1], in_=z[h], axis=AXIS.X, op=ALU.max, negate=True
+        def inverse_of_sum(correction, sums, n):
+            total = small.tile([P, 2], F32, tag="total")
+            for h in range(1, n):
+                nc.vector.scalar_tensor_tensor(
+                    out=total[:, h - 1 : h],
+                    in0=sums[:, 0:1] if h == 1 else total[:, h - 2 : h - 1],
+                    scalar=correction[:, 0:1] if h == 1 else 1.0,
+                    in1=sums[:, h : h + 1],
+                    op0=ALU.mult,
+                    op1=ALU.add,
                 )
-                if h == 0:
-                    exponentials_of(0, neg_maxima[:, 0:1])
-            nc.vector.tensor_reduce(out=neg_max[:], in_=neg_maxima[:], axis=AXIS.X, op=ALU.min)
-            correction = small.tile([P, 1], F32, tag="correction")
-            nc.scalar.activation(
-                out=correction[:], in_=neg_maxima[:, 0:1], func=ACT.Exp, bias=neg_max[:, 0:1], scale=-1.0
-            )
-            normalise_and_store(old[0], old[1], old[2], sum_of_halves(old[3]), True)
-            exponentials_of(1, neg_max[:, 0:1])
-            exponentials_of(2, neg_max[:, 0:1])
-            total = small.tile([P, 1], F32, tag="total")
-            nc.vector.scalar_tensor_tensor(
-                out=sums[:, 3:4], in0=sums[:, 0:1], scalar=correction[:, 0:1], in1=sums[:, 1:2], op0=ALU.mult, op1=ALU.add
-            )
-            nc.vector.tensor_tensor(out=total[:], in0=sums[:, 2:3], in1=sums[:, 3:4], op=ALU.add)
             inverse = small.tile([P, 1], F32, tag="inverse")
-            nc.vector.reciprocal(out=inverse[:], in_=total[:])
-            cut = BANK + BANK // 4
-            nc.scalar.activation(out=e_row[:, cut:E], in_=e_row[:, cut:E], func=ACT.Copy, scale=inverse[:, 0:1])
-            nc.vector.tensor_scalar(
-                out=e_row[:, 0:BANK],
-                in0=e_row[:, 0:BANK],
-                scalar1=correction[:, 0:1],
-                scalar2=inverse[:, 0:1],
+            nc.vector.reciprocal(out=inverse[:], in_=total[:, n - 2 : n - 1])
+            return inverse
+
+        def normalise(engine, e_row, lo, hi, inverse, correction):
+            cols = e_row[:, lo:hi]
+            if engine == "scalar":
+                nc.scalar.activation(out=cols, in_=cols, func=ACT.Copy, scale=inverse[:, 0:1])
+                return
+            builder = nc.vector if engine == "vector" else nc.gpsimd
+            builder.tensor_scalar(
+                out=cols,
+                in0=cols,
+                scalar1=inverse[:, 0:1],
+                scalar2=correction[:, 0:1] if hi <= BANK else 0.0,
                 op0=ALU.mult,
-                op1=ALU.mult,
+                op1=ALU.mult if hi <= BANK else ALU.add,
             )
-            nc.sync.dma_start(out=out_tiles[g, i][:, 0:BANK], in_=e_row[:, 0:BANK])
-            nc.vector.tensor_scalar_mul(out=e_row[:, BANK:cut], in0=e_row[:, BANK:cut], scalar1=inverse[:, 0:1])
-            nc.sync.dma_start(out=out_tiles[g, i][:, BANK:E], in_=e_row[:, BANK:E])
 
         query_tiles = [(g, i) for g in range(GROUPS) for i in range(TILES)]
+        last = len(query_tiles) - 1
         old = None
-        for g, i in query_tiles[:-1]:
-            z = z_passes(g, i)
-            half_max = maxima_of_halves(z)
-            e_row, half_sum = exponentials(z, half_max)
+        for n in range(last + 2):
+            if n <= last:
+                g, i = query_tiles[n]
+                edges = [0, BANK, BANK + BANK // 2, E] if n == last else [0, BANK, E]
+                banks = z_passes(g, i, edges)
+                new = (g, i, len(banks)) + exponentials(banks, edges)
             if old is not None:
-                normalise_and_store(old[0], old[1], old[2], sum_of_halves(old[3]), False)
-            old = (g, i, e_row, half_sum)
-        last_tile(*query_tiles[-1], old)
+                og, oi, count, e_row, correction, sums = old
+                rows_out = out_tiles[og, oi]
+                inverse = inverse_of_sum(correction, sums, count)
+                if n < last:
+                    for lo in (0, BANK):
+                        normalise("gpsimd", e_row, lo, lo + BANK, inverse, correction)
+                        nc.sync.dma_start(out=rows_out[:, lo : lo + BANK], in_=e_row[:, lo : lo + BANK])
+                elif n == last:
+                    for lo, engine in ((0, "vector"), (BANK, "scalar")):
+                        normalise(engine, e_row, lo, lo + BANK, inverse, correction)
+                        nc.sync.dma_start(out=rows_out[:, lo : lo + BANK], in_=e_row[:, lo : lo + BANK])
+                else:
+                    cut = BANK + BANK // 4
+                    normalise("scalar", e_row, cut, E, inverse, correction)
+                    normalise("vector", e_row, 0, BANK, inverse, correction)
+                    nc.sync.dma_start(out=rows_out[:, 0:BANK], in_=e_row[:, 0:BANK])
+                    normalise("vector", e_row, BANK, cut, inverse, correction)
+                    nc.sync.dma_start(out=rows_out[:, BANK:E], in_=e_row[:, BANK:E])
+            old = new

@@ -238,7 +238,44 @@ def tile_headattetion_pa_kernel(tc, qm, km, vm, out):
                 banks.append(bank[:, 0 : hi - lo])
             return banks
 
-        def exponentials(banks, edges):
+        def exponentials(banks):
+            half_max = small.tile([P, HALVES], F32, tag="half_max")
+            for h in range(HALVES):
+                nc.vector.tensor_reduce(
+                    out=half_max[:, h : h + 1], in_=banks[h], axis=AXIS.X, op=ALU.max
+                )
+            neg_max = small.tile([P, 1], F32, tag="neg_max")
+            nc.vector.tensor_reduce(
+                out=neg_max[:], in_=half_max[:], axis=AXIS.X, op=ALU.max, negate=True
+            )
+            e_row = rows.tile([P, E], F32, tag="e_row")
+            half_sum = small.tile([P, HALVES], F32, tag="half_sum")
+            for h in range(HALVES):
+                nc.scalar.activation(
+                    out=e_row[:, h * BANK : (h + 1) * BANK],
+                    in_=banks[h],
+                    func=ACT.Exp,
+                    bias=neg_max[:, 0:1],
+                    scale=1.0,
+                    accum_out=half_sum[:, h : h + 1],
+                )
+            return e_row, half_sum
+
+        def inverse_of_sum(half_sum):
+            total = small.tile([P, 1], F32, tag="total")
+            inverse = small.tile([P, 1], F32, tag="inverse")
+            nc.vector.tensor_reduce(out=total[:], in_=half_sum[:], axis=AXIS.X, op=ALU.add)
+            nc.vector.reciprocal(out=inverse[:], in_=total[:])
+            return inverse
+
+        def normalise_on_gpsimd(g, i, e_row, half_sum):
+            inverse = inverse_of_sum(half_sum)
+            nc.gpsimd.tensor_scalar(
+                out=e_row[:], in0=e_row[:], scalar1=inverse[:, 0:1], scalar2=0.0, op0=ALU.mult, op1=ALU.add
+            )
+            nc.sync.dma_start(out=out_tiles[g, i], in_=e_row[:])
+
+        def early_exponentials(banks, edges):
             n = len(banks)
             neg_maxima = small.tile([P, 4], F32, tag="neg_maxima")
             neg_max = small.tile([P, 1], F32, tag="neg_max")
@@ -271,7 +308,7 @@ def tile_headattetion_pa_kernel(tc, qm, km, vm, out):
                 )
             return e_row, correction, sums
 
-        def inverse_of_sum(correction, sums, n):
+        def corrected_inverse(correction, sums, n):
             total = small.tile([P, 2], F32, tag="total")
             for h in range(1, n):
                 nc.vector.scalar_tensor_tensor(
@@ -290,43 +327,44 @@ def tile_headattetion_pa_kernel(tc, qm, km, vm, out):
             cols = e_row[:, lo:hi]
             if engine == "scalar":
                 nc.scalar.activation(out=cols, in_=cols, func=ACT.Copy, scale=inverse[:, 0:1])
-                return
-            builder = nc.vector if engine == "vector" else nc.gpsimd
-            builder.tensor_scalar(
-                out=cols,
-                in0=cols,
-                scalar1=inverse[:, 0:1],
-                scalar2=correction[:, 0:1] if hi <= BANK else 0.0,
-                op0=ALU.mult,
-                op1=ALU.mult if hi <= BANK else ALU.add,
-            )
+            elif hi <= BANK:
+                nc.vector.tensor_scalar(
+                    out=cols,
+                    in0=cols,
+                    scalar1=inverse[:, 0:1],
+                    scalar2=correction[:, 0:1],
+                    op0=ALU.mult,
+                    op1=ALU.mult,
+                )
+            else:
+                nc.vector.tensor_scalar_mul(out=cols, in0=cols, scalar1=inverse[:, 0:1])
 
         query_tiles = [(g, i) for g in range(GROUPS) for i in range(TILES)]
-        last = len(query_tiles) - 1
-        old = None
-        for n in range(last + 2):
-            if n <= last:
-                g, i = query_tiles[n]
-                edges = [0, BANK, BANK + BANK // 2, E] if n == last else [0, BANK, E]
-                banks = z_passes(g, i, edges)
-                new = (g, i, len(banks)) + exponentials(banks, edges)
-            if old is not None:
-                og, oi, count, e_row, correction, sums = old
-                rows_out = out_tiles[og, oi]
-                inverse = inverse_of_sum(correction, sums, count)
-                if n < last:
-                    for lo in (0, BANK):
-                        normalise("gpsimd", e_row, lo, lo + BANK, inverse, correction)
-                        nc.sync.dma_start(out=rows_out[:, lo : lo + BANK], in_=e_row[:, lo : lo + BANK])
-                elif n == last:
-                    for lo, engine in ((0, "vector"), (BANK, "scalar")):
-                        normalise(engine, e_row, lo, lo + BANK, inverse, correction)
-                        nc.sync.dma_start(out=rows_out[:, lo : lo + BANK], in_=e_row[:, lo : lo + BANK])
-                else:
-                    cut = BANK + BANK // 4
-                    normalise("scalar", e_row, cut, E, inverse, correction)
-                    normalise("vector", e_row, 0, BANK, inverse, correction)
-                    nc.sync.dma_start(out=rows_out[:, 0:BANK], in_=e_row[:, 0:BANK])
-                    normalise("vector", e_row, BANK, cut, inverse, correction)
-                    nc.sync.dma_start(out=rows_out[:, BANK:E], in_=e_row[:, BANK:E])
-            old = new
+        halves = [0, BANK, E]
+        waiting = []
+        for g, i in query_tiles[:-2]:
+            banks = z_passes(g, i, halves)
+            waiting.append((g, i) + exponentials(banks))
+            if len(waiting) > 1:
+                normalise_on_gpsimd(*waiting.pop(0))
+
+        (g, i), (last_g, last_i) = query_tiles[-2:]
+        banks = z_passes(g, i, halves)
+        e_row, correction, sums = early_exponentials(banks, halves)
+        normalise_on_gpsimd(*waiting.pop(0))
+        thirds = [0, BANK, BANK + BANK // 2, E]
+        banks = z_passes(last_g, last_i, thirds)
+        last_e_row, last_correction, last_sums = early_exponentials(banks, thirds)
+        inverse = corrected_inverse(correction, sums, 2)
+        for lo, engine in ((0, "vector"), (BANK, "scalar")):
+            cols = slice(lo, lo + BANK)
+            normalise(engine, e_row, lo, lo + BANK, inverse, correction)
+            nc.sync.dma_start(out=out_tiles[g, i][:, cols], in_=e_row[:, cols])
+        cut = BANK + BANK // 4
+        inverse = corrected_inverse(last_correction, last_sums, 3)
+        rows_out = out_tiles[last_g, last_i]
+        normalise("scalar", last_e_row, cut, E, inverse, last_correction)
+        normalise("vector", last_e_row, 0, BANK, inverse, last_correction)
+        nc.sync.dma_start(out=rows_out[:, 0:BANK], in_=last_e_row[:, 0:BANK])
+        normalise("vector", last_e_row, BANK, cut, inverse, last_correction)
+        nc.sync.dma_start(out=rows_out[:, BANK:E], in_=last_e_row[:, BANK:E])

@@ -24,6 +24,7 @@ GROUPS = S // K_PASS
 TILES = K_PASS // P
 E_PASSES = E // K_PASS
 HALVES = E // BANK
+WARM_UPS = 3
 HEAD = 3
 TILE_WORDS = E // PACK
 
@@ -65,11 +66,13 @@ def tile_headattetion_pa_kernel(tc, qm, km, vm, out):
         for kind, group in needs:
             src = km if kind == "k" else qm
             raw = raw_pool.tile([P, TILES * E], BF16, name="raw_%s%d" % (kind, group), tag="raw")
-            tiles = src[group * K_PASS : (group + 1) * K_PASS, :].rearrange(
-                "(p t) e -> t p e", t=TILES
+            tokens = src[group * K_PASS : (group + 1) * K_PASS, :].rearrange(
+                "(p t) e -> p (t e)", t=TILES
             )
-            for t in range(TILES):
-                nc.sync.dma_start(out=raw[:, t * E : (t + 1) * E], in_=tiles[t])
+            for t, count in ((0, 1), (1, 1), (2, 2)) if not raw_tiles else ((0, 2), (2, 2)):
+                nc.sync.dma_start(
+                    out=raw[:, t * E : (t + count) * E], in_=tokens[:, t * E : (t + count) * E]
+                )
             raw_tiles[(kind, group)] = raw
         for group in range(GROUPS):
             raw = raw_pool.tile([P, TILES * E], BF16, name="raw_v%d" % group, tag="raw")
@@ -87,6 +90,12 @@ def tile_headattetion_pa_kernel(tc, qm, km, vm, out):
         warm = const.tile([P, 1], F32)
         nc.vector.memset(warm[:], 0.0)
         nc.scalar.activation(out=warm[:], in_=warm[:], func=ACT.Exp)
+
+        zeros = const.tile([P, BANK], BF16)
+        nc.vector.memset(zeros[:], 0.0)
+        idle = psum.tile([P, BANK], F32, name="bank_w", tag="bank")
+        for n in range(WARM_UPS):
+            nc.tensor.matmul(idle[:], lhsT=zeros[:, 0:P], rhs=zeros[:], start=True, stop=True)
 
         words = E // 2
         straightened = {}

@@ -25,6 +25,7 @@ TILES = K_PASS // P
 E_PASSES = E // K_PASS
 HALVES = E // BANK
 WARM_UPS = 3
+GPSIMD_COLS = 704
 HEAD = 3
 TILE_WORDS = E // PACK
 
@@ -279,9 +280,12 @@ def tile_headattetion_pa_kernel(tc, qm, km, vm, out):
 
         def normalise_on_gpsimd(g, i, e_row, half_sum):
             inverse = inverse_of_sum(half_sum)
+            cols = e_row[:, 0:GPSIMD_COLS]
             nc.gpsimd.tensor_scalar(
-                out=e_row[:], in0=e_row[:], scalar1=inverse[:, 0:1], scalar2=0.0, op0=ALU.mult, op1=ALU.add
+                out=cols, in0=cols, scalar1=inverse[:, 0:1], scalar2=0.0, op0=ALU.mult, op1=ALU.add
             )
+            cols = e_row[:, GPSIMD_COLS:E]
+            nc.scalar.activation(out=cols, in_=cols, func=ACT.Copy, scale=inverse[:, 0:1])
             nc.sync.dma_start(out=out_tiles[g, i], in_=e_row[:])
 
         def early_exponentials(banks, edges):

@@ -106,8 +106,10 @@ def tile_headattetion_pa_kernel(tc, qm, km, vm, out):
             raw_words = raw_tiles[(kind, group)][:].bitcast(F32)
             tile = straight.tile([P, words], F32, name="straight_t", tag="straight", align_bytes=64)
             nc.vector.tensor_copy(
-                out=tile[:].rearrange("p (u w) -> p u w", u=2),
-                in_=raw_words[:, t * words : (t + 1) * words].rearrange("p (w u) -> p u w", u=2),
+                out=tile[:].rearrange("p (u b i) -> p b u i", u=2, i=4),
+                in_=raw_words[:, t * words : (t + 1) * words].rearrange(
+                    "p (b i u) -> p b u i", i=4, u=2
+                ),
             )
             straightened[(kind, group, t)] = tile
 

import math
from contextlib import ExitStack

import concourse.mybir as mybir
from concourse.masks import make_identity

F32 = mybir.dt.float32
BF16 = mybir.dt.bfloat16
U32 = mybir.dt.uint32
U8 = mybir.dt.uint8
FP8X4 = mybir.dt.float8_e4m3fn_x4
ACT = mybir.ActivationFunctionType
ALU = mybir.AluOpType
AXIS = mybir.AxisListType

S = 1536
E = 1024
P = 128
PACK = 4
K_PASS = P * PACK
BANK = 512

GROUPS = S // K_PASS
TILES = K_PASS // P
E_PASSES = E // K_PASS
HALVES = E // BANK
WARM_UPS = 3
GPSIMD_COLS = 704
HEAD = 3
TILE_WORDS = E // PACK

FLOPS = 2 * S * S * E + 2 * S * S * E


def tile_headattetion_pa_kernel(tc, qm, km, vm, out):
    nc = tc.nc
    inv_sqrt_s = 1.0 / math.sqrt(S)

    with ExitStack() as ctx:
        const = ctx.enter_context(tc.tile_pool(name="const", bufs=1))
        keep = ctx.enter_context(tc.tile_pool(name="keep", bufs=1))
        raw_pool = ctx.enter_context(tc.tile_pool(name="raw", bufs=3 * GROUPS))
        stage = ctx.enter_context(tc.tile_pool(name="stage", bufs=3))
        rows = ctx.enter_context(tc.tile_pool(name="rows", bufs=6))
        small = ctx.enter_context(tc.tile_pool(name="small", bufs=6))
        straight = ctx.enter_context(tc.tile_pool(name="straight", bufs=8))
        psum = ctx.enter_context(tc.psum_pool(name="psum", bufs=8))
        ctx.enter_context(tc.manual_schedule())

        k_codes = keep.tile([P, GROUPS * TILES * TILE_WORDS], U32, align_bytes=64)
        k_scales = keep.tile([P, GROUPS * TILES * TILE_WORDS], U8, align_bytes=64)
        q_codes = keep.tile([P, GROUPS * TILES * TILE_WORDS], U32, align_bytes=64)
        q_scales = keep.tile([P, GROUPS * TILES * TILE_WORDS], U8, align_bytes=64)
        v_codes = keep.tile([P, GROUPS * E], U32, align_bytes=64)
        v_scales = keep.tile([P, GROUPS * E], U8, align_bytes=64)
        s_codes = keep.tile([P, GROUPS * S], U32, align_bytes=64)
        s_scales = keep.tile([P, GROUPS * S], U8, align_bytes=64)

        blocks = [(c, g) for g in range(GROUPS) for c in range(GROUPS)]
        needs = []
        for c, g in blocks:
            for operand in (("k", c), ("q", g)):
                if operand not in needs:
                    needs.append(operand)

        raw_tiles = {}
        for kind, group in needs:
            src = km if kind == "k" else qm
            raw = raw_pool.tile([P, TILES * E], BF16, name="raw_%s%d" % (kind, group), tag="raw")
            tokens = src[group * K_PASS : (group + 1) * K_PASS, :].rearrange(
                "(p t) e -> p (t e)", t=TILES
            )
            for t, count in ((0, 1), (1, 1), (2, 2)) if not raw_tiles else ((0, 2), (2, 2)):
                nc.sync.dma_start(
                    out=raw[:, t * E : (t + count) * E], in_=tokens[:, t * E : (t + count) * E]
                )
            raw_tiles[(kind, group)] = raw
        for group in range(GROUPS):
            raw = raw_pool.tile([P, TILES * E], BF16, name="raw_v%d" % group, tag="raw")
            nc.sync.dma_start(
                out=raw[:],
                in_=vm[group * K_PASS : (group + 1) * K_PASS, :].rearrange(
                    "(p t) e -> p (t e)", t=TILES
                ),
            )
            raw_tiles[("v", group)] = raw

        ident = const.tile([P, P], F32)
        make_identity(nc, ident[:])

        warm = const.tile([P, 1], F32)
        nc.vector.memset(warm[:], 0.0)
        nc.scalar.activation(out=warm[:], in_=warm[:], func=ACT.Exp)

        zeros = const.tile([P, BANK], BF16)
        nc.vector.memset(zeros[:], 0.0)
        idle = psum.tile([P, BANK], F32, name="bank_w", tag="bank")
        for n in range(WARM_UPS):
            nc.tensor.matmul(idle[:], lhsT=zeros[:, 0:P], rhs=zeros[:], start=True, stop=True)

        words = E // 2
        straightened = {}
        grouped_tiles = {}

        def straighten(kind, group, t):
            raw_words = raw_tiles[(kind, group)][:].bitcast(F32)
            tile = straight.tile([P, words], F32, name="straight_t", tag="straight", align_bytes=64)
            nc.vector.tensor_copy(
                out=tile[:].rearrange("p (u b i) -> p b u i", u=2, i=4),
                in_=raw_words[:, t * words : (t + 1) * words].rearrange(
                    "p (b i u) -> p b u i", i=4, u=2
                ),
            )
            straightened[(kind, group, t)] = tile

        def transpose_tile(kind, group, t):
            raw_words = raw_tiles[(kind, group)][:].bitcast(F32)
            if t == 0:
                grouped_tiles[(kind, group)] = stage.tile(
                    [P, TILES * E], BF16, name="grouped", tag="grouped", align_bytes=64
                )
            grouped_words = grouped_tiles[(kind, group)][:].bitcast(F32)
            bank = psum.tile([P, BANK], F32, name="bank_t", tag="bank")
            for j in range(words // P):
                a, u = j // 2, j % 2
                if (kind, group, t) in straightened:
                    first = u * (words // 2) + a * P
                    in_ = straightened[(kind, group, t)][:, first : first + P]
                else:
                    first = t * words + 2 * P * a + u
                    in_ = raw_words[:, first : first + 2 * P - 1 : 2]
                nc.tensor.transpose(bank[:, j * P : (j + 1) * P], in_, ident[:])
            copy = nc.scalar.copy if ("V" if t == 0 and (kind, group) not in needs[: HEAD - 1] else "S") == "S" else nc.vector.tensor_copy
            copy(
                out=grouped_words[:, t * words : (t + 1) * words].rearrange(
                    "p (a r u) -> p a r u", a=E_PASSES, u=2
                ),
                in_=bank[:].rearrange("p (a u r) -> p a r u", a=E_PASSES, u=2),
            )

        def quantise_tile(kind, group, t):
            codes, scales = (k_codes, k_scales) if kind == "k" else (q_codes, q_scales)
            first = (group * TILES + t) * TILE_WORDS
            nc.vector.quantize_mx(
                out=codes[:, first : first + TILE_WORDS].bitcast(FP8X4),
                scales=scales[:, first : first + TILE_WORDS],
                in_=grouped_tiles[(kind, group)][:, t * E : (t + 1) * E],
            )

        def score_block(c, g):
            s_grouped = stage.tile([P, TILES * P * PACK], BF16, tag="s_grouped", align_bytes=64)
            for i in range(TILES):
                bank = psum.tile([P, BANK], F32, name="bank_s", tag="bank")
                for t in range(TILES):
                    for a in range(E_PASSES):
                        k_first = (c * TILES + t) * TILE_WORDS + a * P
                        q_first = (g * TILES + i) * TILE_WORDS + a * P
                        nc.tensor.matmul_mx(
                            out=bank[:, t * P : (t + 1) * P],
                            lhsT=k_codes[:, k_first : k_first + P].bitcast(FP8X4),
                            lhsT_scale=k_scales[:, k_first : k_first + P],
                            rhs=q_codes[:, q_first : q_first + P].bitcast(FP8X4),
                            rhs_scale=q_scales[:, q_first : q_first + P],
                            start=(a == 0),
                            stop=(a == E_PASSES - 1),
                        )
                nc.scalar.activation(
                    out=s_grouped[:, i * BANK : (i + 1) * BANK].rearrange(
                        "p (n t) -> p n t", t=TILES
                    ),
                    in_=bank[:].rearrange("p (t n) -> p n t", t=TILES),
                    func=ACT.Copy,
                    scale=inv_sqrt_s,
                )
            return s_grouped

        def quantise_block(c, g, s_grouped):
            first = (c * GROUPS + g) * K_PASS
            nc.vector.quantize_mx(
                out=s_codes[:, first : first + K_PASS].bitcast(FP8X4),
                scales=s_scales[:, first : first + K_PASS],
                in_=s_grouped[:],
            )

        def regroup_v(c, h):
            v_grouped = stage.tile([P, BANK * PACK], BF16, tag="v_grouped", align_bytes=64)
            src = raw_tiles[("v", c)][:].rearrange("p (t f) -> p t f", t=TILES)
            nc.vector.tensor_copy(
                out=v_grouped[:].rearrange("p (b i t) -> p b t i", i=4, t=TILES),
                in_=src[:, :, h * BANK : (h + 1) * BANK].rearrange("p t (b i) -> p b t i", i=4),
            )
            return v_grouped

        def quantise_v(c, h, v_grouped):
            first = c * E + h * BANK
            nc.vector.quantize_mx(
                out=v_codes[:, first : first + BANK].bitcast(FP8X4),
                scales=v_scales[:, first : first + BANK],
                in_=v_grouped[:],
            )

        v_pieces = [(c, h) for c in range(GROUPS) for h in range(HALVES)]
        head_tiles = [need + (t,) for need in needs[:HEAD] for t in range(TILES)]
        for m, tile in enumerate(head_tiles):
            transpose_tile(*tile)
            if m >= 2:
                quantise_tile(*head_tiles[m - 2])
        for tile in head_tiles[-2:]:
            quantise_tile(*tile)
        waiting = None
        for b, (c, g) in enumerate(blocks):
            ahead = needs[b + 2] if HEAD <= b + 2 < len(needs) else None
            if ahead:
                for t in range(TILES):
                    transpose_tile(*ahead, t)
            s_grouped = score_block(c, g)
            piece = b - (len(blocks) - len(v_pieces))
            if piece >= 0:
                v_grouped = regroup_v(*v_pieces[piece])
            if waiting is not None:
                quantise_block(*waiting)
            if ahead:
                for t in range(TILES):
                    quantise_tile(*ahead, t)
            if piece >= 0:
                quantise_v(*v_pieces[piece], v_grouped)
            if HEAD <= b + 3 < len(needs):
                for t in range(TILES):
                    straighten(*needs[b + 3], t)
            waiting = (c, g, s_grouped)
        quantise_block(*waiting)

        out_tiles = out.rearrange("(g p t) f -> g t p f", p=P, t=TILES)

        def z_passes(g, i, edges):
            banks = []
            for lo, hi in zip(edges, edges[1:]):
                bank = psum.tile([P, BANK], F32, name="bank_z", tag="bank")
                for c in range(GROUPS):
                    s_first = (c * GROUPS + g) * K_PASS + i * P
                    nc.tensor.matmul_mx(
                        out=bank[:, 0 : hi - lo],
                        lhsT=s_codes[:, s_first : s_first + P].bitcast(FP8X4),
                        lhsT_scale=s_scales[:, s_first : s_first + P],
                        rhs=v_codes[:, c * E + lo : c * E + hi].bitcast(FP8X4),
                        rhs_scale=v_scales[:, c * E + lo : c * E + hi],
                        start=(c == 0),
                        stop=(c == GROUPS - 1),
                    )
                banks.append(bank[:, 0 : hi - lo])
            return banks

        def exponentials(banks):
            half_max = small.tile([P, HALVES], F32, tag="half_max")
            for h in range(HALVES):
                nc.vector.tensor_reduce(
                    out=half_max[:, h : h + 1], in_=banks[h], axis=AXIS.X, op=ALU.max
                )
            neg_max = small.tile([P, 1], F32, tag="neg_max")
            nc.vector.tensor_reduce(
                out=neg_max[:], in_=half_max[:], axis=AXIS.X, op=ALU.max, negate=True
            )
            e_row = rows.tile([P, E], F32, tag="e_row")
            half_sum = small.tile([P, HALVES], F32, tag="half_sum")
            for h in range(HALVES):
                nc.scalar.activation(
                    out=e_row[:, h * BANK : (h + 1) * BANK],
                    in_=banks[h],
                    func=ACT.Exp,
                    bias=neg_max[:, 0:1],
                    scale=1.0,
                    accum_out=half_sum[:, h : h + 1],
                )
            return e_row, half_sum

        def inverse_of_sum(half_sum):
            total = small.tile([P, 1], F32, tag="total")
            inverse = small.tile([P, 1], F32, tag="inverse")
            nc.vector.tensor_reduce(out=total[:], in_=half_sum[:], axis=AXIS.X, op=ALU.add)
            nc.vector.reciprocal(out=inverse[:], in_=total[:])
            return inverse

        def normalise_on_gpsimd(g, i, e_row, half_sum):
            inverse = inverse_of_sum(half_sum)
            cols = e_row[:, 0:GPSIMD_COLS]
            nc.gpsimd.tensor_scalar(
                out=cols, in0=cols, scalar1=inverse[:, 0:1], scalar2=0.0, op0=ALU.mult, op1=ALU.add
            )
            cols = e_row[:, GPSIMD_COLS:E]
            nc.scalar.activation(out=cols, in_=cols, func=ACT.Copy, scale=inverse[:, 0:1])
            nc.sync.dma_start(out=out_tiles[g, i], in_=e_row[:])

        def early_exponentials(banks, edges):
            n = len(banks)
            neg_maxima = small.tile([P, 4], F32, tag="neg_maxima")
            neg_max = small.tile([P, 1], F32, tag="neg_max")
            correction = small.tile([P, 1], F32, tag="correction")
            sums = small.tile([P, 4], F32, tag="sums")
            e_row = rows.tile([P, E], F32, tag="e_row")
            for h in range(n):
                nc.vector.tensor_reduce(
                    out=neg_maxima[:, h : h + 1], in_=banks[h], axis=AXIS.X, op=ALU.max, negate=True
                )
            nc.vector.tensor_reduce(
                out=neg_max[:], in_=neg_maxima[:, 0:n], axis=AXIS.X, op=ALU.min
            )
            for h in range(n):
                if h == 1:
                    nc.scalar.activation(
                        out=correction[:],
                        in_=neg_maxima[:, 0:1],
                        func=ACT.Exp,
                        bias=neg_max[:, 0:1],
                        scale=-1.0,
                    )
                nc.scalar.activation(
                    out=e_row[:, edges[h] : edges[h + 1]],
                    in_=banks[h],
                    func=ACT.Exp,
                    bias=neg_maxima[:, 0:1] if h == 0 else neg_max[:, 0:1],
                    scale=1.0,
                    accum_out=sums[:, h : h + 1],
                )
            return e_row, correction, sums

        def corrected_inverse(correction, sums, n):
            total = small.tile([P, 2], F32, tag="total")
            for h in range(1, n):
                nc.vector.scalar_tensor_tensor(
                    out=total[:, h - 1 : h],
                    in0=sums[:, 0:1] if h == 1 else total[:, h - 2 : h - 1],
                    scalar=correction[:, 0:1] if h == 1 else 1.0,
                    in1=sums[:, h : h + 1],
                    op0=ALU.mult,
                    op1=ALU.add,
                )
            inverse = small.tile([P, 1], F32, tag="inverse")
            nc.vector.reciprocal(out=inverse[:], in_=total[:, n - 2 : n - 1])
            return inverse

        def normalise(engine, e_row, lo, hi, inverse, correction):
            cols = e_row[:, lo:hi]
            if engine == "scalar":
                nc.scalar.activation(out=cols, in_=cols, func=ACT.Copy, scale=inverse[:, 0:1])
            elif hi <= BANK:
                nc.vector.tensor_scalar(
                    out=cols,
                    in0=cols,
                    scalar1=inverse[:, 0:1],
                    scalar2=correction[:, 0:1],
                    op0=ALU.mult,
                    op1=ALU.mult,
                )
            else:
                nc.vector.tensor_scalar_mul(out=cols, in0=cols, scalar1=inverse[:, 0:1])

        query_tiles = [(g, i) for g in range(GROUPS) for i in range(TILES)]
        halves = [0, BANK, E]
        waiting = []
        for g, i in query_tiles[:-2]:
            banks = z_passes(g, i, halves)
            waiting.append((g, i) + exponentials(banks))
            if len(waiting) > 1:
                normalise_on_gpsimd(*waiting.pop(0))

        (g, i), (last_g, last_i) = query_tiles[-2:]
        banks = z_passes(g, i, halves)
        e_row, correction, sums = early_exponentials(banks, halves)
        normalise_on_gpsimd(*waiting.pop(0))
        thirds = [0, BANK, BANK + BANK // 2, E]
        banks = z_passes(last_g, last_i, thirds)
        last_e_row, last_correction, last_sums = early_exponentials(banks, thirds)
        inverse = corrected_inverse(correction, sums, 2)
        for lo, engine in ((0, "vector"), (BANK, "scalar")):
            cols = slice(lo, lo + BANK)
            normalise(engine, e_row, lo, lo + BANK, inverse, correction)
            nc.sync.dma_start(out=out_tiles[g, i][:, cols], in_=e_row[:, cols])
        cut = BANK + BANK // 4
        inverse = corrected_inverse(last_correction, last_sums, 3)
        rows_out = out_tiles[last_g, last_i]
        normalise("scalar", last_e_row, cut, E, inverse, last_correction)
        normalise("vector", last_e_row, 0, BANK, inverse, last_correction)
        nc.sync.dma_start(out=rows_out[:, 0:BANK], in_=last_e_row[:, 0:BANK])
        normalise("vector", last_e_row, BANK, cut, inverse, last_correction)
        nc.sync.dma_start(out=rows_out[:, BANK:E], in_=last_e_row[:, BANK:E])
